import numpy as np
import ml_dtypes


def mxq(x, axis, fmt="e4m3"):
    dtype, down = {"e4m3": (ml_dtypes.float8_e4m3fn, 7), "e5m2": (ml_dtypes.float8_e5m2, 14)}[fmt]
    v = np.moveaxis(np.asarray(x, np.float32).astype(ml_dtypes.bfloat16).astype(np.float64), axis, -1)
    blocks = v.reshape(v.shape[:-1] + (-1, 32))
    amax = np.abs(blocks).max(-1, keepdims=True)
    byte = np.maximum(np.where(amax > 0, np.frexp(amax)[1] - 1 + 127, 0) - down, 1)
    scale = np.exp2(byte - 127.0)
    codes = (blocks / scale).astype(np.float32).astype(dtype).astype(np.float64)
    return np.moveaxis((codes * scale).reshape(v.shape), -1, axis)


WIDE = False


def mx_kscale(k):
    if not WIDE:
        return np.ones(k)
    levels = np.array([20, -20, 10, -10, 0])
    a = np.random.permutation(np.resize(levels, k // 512 * 4)).reshape(k // 512, 4)
    idx = np.arange(k)
    return np.exp2(a[idx // 512, idx % 128 // 32])


BF16 = ml_dtypes.bfloat16


def bf(x):
    return np.asarray(x, np.float32).astype(BF16)


def f64(x):
    return np.asarray(x).astype(np.float64)


B, T, C, R, H, DN, DR, DV = 2, 256, 2048, 512, 16, 128, 64, 128
DQ = DN + DR
NF = DR // 2


def rotate_half(u):
    u1, u2 = u[..., : u.shape[-1] // 2], u[..., u.shape[-1] // 2 :]
    return np.concatenate([-u2, u1], axis=-1)


def setup_inputs():
    u = np.array(mx_kscale(H * DQ), dtype=np.float64).reshape(H, DQ)
    u[:, DN + NF :] = u[:, DN : DN + NF]
    x = np.random.standard_normal((B, T, C))
    freqs_cis = np.stack([np.random.uniform(size=(T, NF)), np.random.uniform(size=(T, NF))], axis=-1)
    w_q = np.random.standard_normal((C, H * DQ)) / np.sqrt(C) / u.reshape(1, H * DQ)
    g = np.random.standard_normal((B, T, H, DQ)) * np.exp2(np.random.randint(-12, 1, (B, T, 1, 1))) * 4.0 * u
    return {"x": bf(x), "freqs_cis": bf(freqs_cis), "w_q": bf(w_q), "grad_out": bf(g)}


def reference(x, freqs_cis, w_q, grad_out):
    g = f64(grad_out)
    freqs = f64(freqs_cis)
    cos = freqs[..., 0][None, :, None, :]
    sin = freqs[..., 1][None, :, None, :]
    g1 = g[..., DN : DN + NF]
    g2 = g[..., DN + NF :]
    gq = np.concatenate([g[..., :DN], g1 * cos + g2 * sin, g2 * cos - g1 * sin], axis=-1).reshape(B, T, H * DQ)
    return mxq(gq, 2, "e5m2") @ mxq(f64(w_q), 1, "e4m3").T

@@ -1,0 +1,134 @@
+from contextlib import ExitStack
+
+import concourse.mybir as mybir
+from concourse.masks import make_identity
+
+F32 = mybir.dt.float32
+BF16 = mybir.dt.bfloat16
+U32 = mybir.dt.uint32
+U8 = mybir.dt.uint8
+E4M3_X4 = mybir.dt.float8_e4m3fn_x4
+E5M2_X4 = mybir.dt.float8_e5m2_x4
+
+P = 128
+TOKENS = 512
+POSITIONS = 256
+HEADS = 16
+PLAIN = 128
+NF = 32
+HEAD = PLAIN + 2 * NF
+K = HEADS * HEAD
+C = 2048
+K_PASS = 4 * P
+PASSES = K // K_PASS
+N_BLOCK = 512
+TOKEN_TILES = TOKENS // P
+C_TILES = C // P
+C_TILES_PER_BLOCK = N_BLOCK // P
+
+FLOPS = 2 * TOKENS * C * K
+BYTES = 2 * C * K + 2 * TOKENS * K + 2 * POSITIONS * NF * 2 + 4 * TOKENS * C
+
+
+def undo_rotation(nc, work, rows, cos, sin):
+    shape = [P, HEADS, 2, NF]
+    rotated = rows.rearrange("p (h d) -> p h d", d=HEAD)[:, :, PLAIN:HEAD].rearrange(
+        "p h (f j) -> p h f j", f=2
+    )
+    by_cos = work.tile(shape, F32)
+    by_sin = work.tile(shape, F32)
+    nc.vector.tensor_mul(out=by_cos[:], in0=rotated, in1=cos.unsqueeze(1).unsqueeze(1).to_broadcast(shape))
+    nc.gpsimd.tensor_mul(out=by_sin[:], in0=rotated, in1=sin.unsqueeze(1).unsqueeze(1).to_broadcast(shape))
+    nc.vector.tensor_add(out=rotated[:, :, 0, :], in0=by_cos[:, :, 0, :], in1=by_sin[:, :, 1, :])
+    nc.vector.tensor_sub(out=rotated[:, :, 1, :], in0=by_cos[:, :, 1, :], in1=by_sin[:, :, 0, :])
+
+
+def k_onto_partitions(nc, banks, identity, rows, grouped):
+    words = rows.bitcast(F32).rearrange("p (g w u) -> p g u w", g=PASSES, u=2)
+    grouped_words = grouped.bitcast(F32).rearrange("p g (r u) -> p g r u", u=2)
+    for b in range(PASSES // 2):
+        bank = banks.tile([P, 2, 2, P], F32)
+        for g in range(2):
+            for u in range(2):
+                nc.tensor.transpose(bank[:, g, u, :], words[:, 2 * b + g, u, :], identity)
+        paired = bank[:].rearrange("p g u r -> p g r u")
+        if b == 2:
+            nc.vector.tensor_copy(out=grouped_words[:, 2 * b : 2 * b + 2, :, :], in_=paired)
+        else:
+            nc.scalar.copy(out=grouped_words[:, 2 * b : 2 * b + 2, :, :], in_=paired)
+
+
+def tile_fa3mlaattention_pb_kernel(tc, x, freqs_cis, w_q, grad_out, out):
+    nc = tc.nc
+    g_dram = grad_out.rearrange("b t h d -> (b t) (h d)")
+    out_dram = out.rearrange("b t c -> (b t) c")
+
+    with ExitStack() as ctx:
+        keep = ctx.enter_context(tc.tile_pool(name="keep", bufs=1))
+        work = ctx.enter_context(tc.tile_pool(name="work", bufs=2))
+        stage = ctx.enter_context(tc.tile_pool(name="stage", bufs=3))
+        banks = ctx.enter_context(tc.psum_pool(name="banks", bufs=6))
+        sums = ctx.enter_context(tc.psum_pool(name="sums", bufs=2))
+
+        freqs = keep.tile([P, POSITIONS // P, NF, 2], BF16)
+        nc.sync.dma_start(out=freqs[:], in_=freqs_cis.rearrange("(a p) j s -> p a j s", p=P))
+        g_rows = keep.tile([P, TOKEN_TILES, K], BF16)
+        for tt in range(TOKEN_TILES):
+            nc.sync.dma_start(out=g_rows[:, tt, :], in_=g_dram[tt * P : (tt + 1) * P, :])
+        w_rows = keep.tile([P, C_TILES, K], BF16)
+        for ct in range(C_TILES):
+            nc.sync.dma_start(out=w_rows[:, ct, :], in_=w_q[ct * P : (ct + 1) * P, :])
+
+        identity = keep.tile([P, P], F32)
+        make_identity(nc, identity[:])
+
+        gq_codes = keep.tile([P, TOKEN_TILES, PASSES, P], U32, align_bytes=64)
+        gq_scales = keep.tile([P, TOKEN_TILES, PASSES, P], U8, align_bytes=64)
+        for tt in range(TOKEN_TILES):
+            a = tt % (POSITIONS // P)
+            undo_rotation(nc, work, g_rows[:, tt, :], freqs[:, a, :, 0], freqs[:, a, :, 1])
+            gq_grouped = stage.tile([P, PASSES, 4 * P], BF16, align_bytes=64, tag="grouped")
+            k_onto_partitions(nc, banks, identity[:], g_rows[:, tt, :], gq_grouped[:])
+            for b in range(PASSES // 2):
+                two = slice(2 * b, 2 * b + 2)
+                nc.vector.quantize_mx(
+                    out=gq_codes[:, tt, two, :].rearrange("p g r -> p (g r)").bitcast(E5M2_X4),
+                    scales=gq_scales[:, tt, two, :].rearrange("p g r -> p (g r)"),
+                    in_=gq_grouped[:, two, :].rearrange("p g e -> p (g e)"),
+                )
+
+        w_codes = {}
+        w_scales = {}
+        for step in range(C_TILES + C_TILES_PER_BLOCK):
+            cb, i = divmod(step, C_TILES_PER_BLOCK)
+            if step < C_TILES:
+                if i == 0:
+                    w_codes[cb] = stage.tile([P, PASSES, N_BLOCK], U32, align_bytes=64, name="w_codes", bufs=2)
+                    w_scales[cb] = stage.tile([P, PASSES, N_BLOCK], U8, align_bytes=64, name="w_scales", bufs=2)
+                w_grouped = stage.tile([P, PASSES, 4 * P], BF16, align_bytes=64, tag="grouped")
+                k_onto_partitions(nc, banks, identity[:], w_rows[:, step, :], w_grouped[:])
+                cols = slice(i * P, (i + 1) * P)
+                for g in range(PASSES):
+                    nc.vector.quantize_mx(
+                        out=w_codes[cb][:, g, cols].bitcast(E4M3_X4),
+                        scales=w_scales[cb][:, g, cols],
+                        in_=w_grouped[:, g, :],
+                    )
+            if cb >= 1:
+                done, tt = cb - 1, i
+                acc = sums.tile([P, N_BLOCK], F32)
+                for g in range(PASSES):
+                    nc.tensor.matmul_mx(
+                        out=acc[:],
+                        lhsT=gq_codes[:, tt, g, :].bitcast(E5M2_X4),
+                        lhsT_scale=gq_scales[:, tt, g, :],
+                        rhs=w_codes[done][:, g, :].bitcast(E4M3_X4),
+                        rhs_scale=w_scales[done][:, g, :],
+                        start=(g == 0),
+                        stop=(g == PASSES - 1),
+                    )
+                result = stage.tile([P, N_BLOCK], F32)
+                nc.scalar.copy(out=result[:], in_=acc[:])
+                nc.sync.dma_start(
+                    out=out_dram[tt * P : (tt + 1) * P, done * N_BLOCK : (done + 1) * N_BLOCK], in_=result[:]
+                )

@@ -43,19 +43,16 @@ def undo_rotation(nc, work, rows, cos, sin):
     nc.vector.tensor_sub(out=rotated[:, :, 1, :], in0=by_cos[:, :, 1, :], in1=by_sin[:, :, 0, :])
 
 
-def k_onto_partitions(nc, banks, identity, rows, grouped):
-    words = rows.bitcast(F32).rearrange("p (g w u) -> p g u w", g=PASSES, u=2)
+def k_onto_partitions(nc, banks, identity, words, grouped):
     grouped_words = grouped.bitcast(F32).rearrange("p g (r u) -> p g r u", u=2)
     for b in range(PASSES // 2):
         bank = banks.tile([P, 2, 2, P], F32)
         for g in range(2):
             for u in range(2):
                 nc.tensor.transpose(bank[:, g, u, :], words[:, 2 * b + g, u, :], identity)
-        paired = bank[:].rearrange("p g u r -> p g r u")
-        if b == 2:
-            nc.vector.tensor_copy(out=grouped_words[:, 2 * b : 2 * b + 2, :, :], in_=paired)
-        else:
-            nc.scalar.copy(out=grouped_words[:, 2 * b : 2 * b + 2, :, :], in_=paired)
+        nc.scalar.copy(
+            out=grouped_words[:, 2 * b : 2 * b + 2, :, :], in_=bank[:].rearrange("p g u r -> p g r u")
+        )
 
 
 def tile_fa3mlaattention_pb_kernel(tc, x, freqs_cis, w_q, grad_out, out):
@@ -88,7 +85,8 @@ def tile_fa3mlaattention_pb_kernel(tc, x, freqs_cis, w_q, grad_out, out):
             a = tt % (POSITIONS // P)
             undo_rotation(nc, work, g_rows[:, tt, :], freqs[:, a, :, 0], freqs[:, a, :, 1])
             gq_grouped = stage.tile([P, PASSES, 4 * P], BF16, align_bytes=64, tag="grouped")
-            k_onto_partitions(nc, banks, identity[:], g_rows[:, tt, :], gq_grouped[:])
+            gq_words = g_rows[:, tt, :].bitcast(F32).rearrange("p (g w u) -> p g u w", g=PASSES, u=2)
+            k_onto_partitions(nc, banks, identity[:], gq_words, gq_grouped[:])
             for b in range(PASSES // 2):
                 two = slice(2 * b, 2 * b + 2)
                 nc.vector.quantize_mx(
@@ -106,7 +104,12 @@ def tile_fa3mlaattention_pb_kernel(tc, x, freqs_cis, w_q, grad_out, out):
                     w_codes[cb] = stage.tile([P, PASSES, N_BLOCK], U32, align_bytes=64, name="w_codes", bufs=2)
                     w_scales[cb] = stage.tile([P, PASSES, N_BLOCK], U8, align_bytes=64, name="w_scales", bufs=2)
                 w_grouped = stage.tile([P, PASSES, 4 * P], BF16, align_bytes=64, tag="grouped")
-                k_onto_partitions(nc, banks, identity[:], w_rows[:, step, :], w_grouped[:])
+                w_sorted = stage.tile([P, 2, K // 4], F32)
+                nc.vector.tensor_copy(
+                    out=w_sorted[:], in_=w_rows[:, step, :].bitcast(F32).rearrange("p (w u) -> p u w", u=2)
+                )
+                w_words = w_sorted[:].rearrange("p u (g w) -> p g u w", g=PASSES)
+                k_onto_partitions(nc, banks, identity[:], w_words, w_grouped[:])
                 cols = slice(i * P, (i + 1) * P)
                 for g in range(PASSES):
                     nc.vector.quantize_mx(

@@ -25,6 +25,10 @@ N_BLOCK = 512
 TOKEN_TILES = TOKENS // P
 C_TILES = C // P
 C_TILES_PER_BLOCK = N_BLOCK // P
+PRODUCTS = TOKEN_TILES * (C // N_BLOCK)
+
+PRODUCT_LAG = 2
+UNSORTED_TILES = 6
 
 FLOPS = 2 * TOKENS * C * K
 BYTES = 2 * C * K + 2 * TOKENS * K + 2 * POSITIONS * NF * 2 + 4 * TOKENS * C
@@ -38,7 +42,7 @@ def undo_rotation(nc, work, rows, cos, sin):
     by_cos = work.tile(shape, F32)
     by_sin = work.tile(shape, F32)
     nc.vector.tensor_mul(out=by_cos[:], in0=rotated, in1=cos.unsqueeze(1).unsqueeze(1).to_broadcast(shape))
-    nc.gpsimd.tensor_mul(out=by_sin[:], in0=rotated, in1=sin.unsqueeze(1).unsqueeze(1).to_broadcast(shape))
+    nc.vector.tensor_mul(out=by_sin[:], in0=rotated, in1=sin.unsqueeze(1).unsqueeze(1).to_broadcast(shape))
     nc.vector.tensor_add(out=rotated[:, :, 0, :], in0=by_cos[:, :, 0, :], in1=by_sin[:, :, 1, :])
     nc.vector.tensor_sub(out=rotated[:, :, 1, :], in0=by_cos[:, :, 1, :], in1=by_sin[:, :, 0, :])
 
@@ -61,77 +65,93 @@ def tile_fa3mlaattention_pb_kernel(tc, x, freqs_cis, w_q, grad_out, out):
     out_dram = out.rearrange("b t c -> (b t) c")
 
     with ExitStack() as ctx:
+        ctx.enter_context(tc.manual_schedule())
         keep = ctx.enter_context(tc.tile_pool(name="keep", bufs=1))
-        work = ctx.enter_context(tc.tile_pool(name="work", bufs=2))
-        stage = ctx.enter_context(tc.tile_pool(name="stage", bufs=3))
+        stage = ctx.enter_context(tc.tile_pool(name="stage", bufs=2))
         banks = ctx.enter_context(tc.psum_pool(name="banks", bufs=6))
         sums = ctx.enter_context(tc.psum_pool(name="sums", bufs=2))
 
         freqs = keep.tile([P, POSITIONS // P, NF, 2], BF16)
         nc.sync.dma_start(out=freqs[:], in_=freqs_cis.rearrange("(a p) j s -> p a j s", p=P))
         g_rows = keep.tile([P, TOKEN_TILES, K], BF16)
-        for tt in range(TOKEN_TILES):
-            nc.sync.dma_start(out=g_rows[:, tt, :], in_=g_dram[tt * P : (tt + 1) * P, :])
         w_rows = keep.tile([P, C_TILES, K], BF16)
-        for ct in range(C_TILES):
-            nc.sync.dma_start(out=w_rows[:, ct, :], in_=w_q[ct * P : (ct + 1) * P, :])
+        for r in range(C_TILES):
+            if r < TOKEN_TILES:
+                nc.sync.dma_start(out=g_rows[:, r, :], in_=g_dram[r * P : (r + 1) * P, :])
+            nc.sync.dma_start(out=w_rows[:, r, :], in_=w_q[r * P : (r + 1) * P, :])
 
         identity = keep.tile([P, P], F32)
         make_identity(nc, identity[:])
 
         gq_codes = keep.tile([P, TOKEN_TILES, PASSES, P], U32, align_bytes=64)
         gq_scales = keep.tile([P, TOKEN_TILES, PASSES, P], U8, align_bytes=64)
-        for tt in range(TOKEN_TILES):
-            a = tt % (POSITIONS // P)
-            undo_rotation(nc, work, g_rows[:, tt, :], freqs[:, a, :, 0], freqs[:, a, :, 1])
-            gq_grouped = stage.tile([P, PASSES, 4 * P], BF16, align_bytes=64, tag="grouped")
-            gq_words = g_rows[:, tt, :].bitcast(F32).rearrange("p (g w u) -> p g u w", g=PASSES, u=2)
-            k_onto_partitions(nc, banks, identity[:], gq_words, gq_grouped[:])
-            for b in range(PASSES // 2):
-                two = slice(2 * b, 2 * b + 2)
-                nc.vector.quantize_mx(
-                    out=gq_codes[:, tt, two, :].rearrange("p g r -> p (g r)").bitcast(E5M2_X4),
-                    scales=gq_scales[:, tt, two, :].rearrange("p g r -> p (g r)"),
-                    in_=gq_grouped[:, two, :].rearrange("p g e -> p (g e)"),
-                )
-
         w_codes = {}
         w_scales = {}
-        for step in range(C_TILES + C_TILES_PER_BLOCK):
-            cb, i = divmod(step, C_TILES_PER_BLOCK)
-            if step < C_TILES:
-                if i == 0:
-                    w_codes[cb] = stage.tile([P, PASSES, N_BLOCK], U32, align_bytes=64, name="w_codes", bufs=2)
-                    w_scales[cb] = stage.tile([P, PASSES, N_BLOCK], U8, align_bytes=64, name="w_scales", bufs=2)
-                w_grouped = stage.tile([P, PASSES, 4 * P], BF16, align_bytes=64, tag="grouped")
+        w_words = {}
+        w_grouped = {}
+        gq_grouped = {}
+
+        for r in range(C_TILES + PRODUCT_LAG + C_TILES_PER_BLOCK - 1):
+            if r < TOKEN_TILES:
+                a = r % (POSITIONS // P)
+                undo_rotation(nc, keep, g_rows[:, r, :], freqs[:, a, :, 0], freqs[:, a, :, 1])
+
+            ahead = r + 1
+            if UNSORTED_TILES <= ahead < C_TILES:
                 w_sorted = stage.tile([P, 2, K // 4], F32)
                 nc.vector.tensor_copy(
-                    out=w_sorted[:], in_=w_rows[:, step, :].bitcast(F32).rearrange("p (w u) -> p u w", u=2)
+                    out=w_sorted[:], in_=w_rows[:, ahead, :].bitcast(F32).rearrange("p (w u) -> p u w", u=2)
                 )
-                w_words = w_sorted[:].rearrange("p u (g w) -> p g u w", g=PASSES)
-                k_onto_partitions(nc, banks, identity[:], w_words, w_grouped[:])
+                w_words[ahead] = w_sorted[:].rearrange("p u (g w) -> p g u w", g=PASSES)
+
+            if r < C_TILES:
+                if r < UNSORTED_TILES:
+                    w_words[r] = w_rows[:, r, :].bitcast(F32).rearrange("p (g w u) -> p g u w", g=PASSES, u=2)
+                w_grouped[r] = stage.tile([P, PASSES, 4 * P], BF16, align_bytes=64, name="w_grouped")
+                k_onto_partitions(nc, banks, identity[:], w_words[r], w_grouped[r][:])
+            if r < TOKEN_TILES:
+                gq_words = g_rows[:, r, :].bitcast(F32).rearrange("p (g w u) -> p g u w", g=PASSES, u=2)
+                gq_grouped[r] = stage.tile([P, PASSES, 4 * P], BF16, align_bytes=64, name="gq_grouped")
+                k_onto_partitions(nc, banks, identity[:], gq_words, gq_grouped[r][:])
+
+            before = r - 1
+            if 0 <= before < C_TILES:
+                cb, i = divmod(before, C_TILES_PER_BLOCK)
+                if i == 0:
+                    w_codes[cb] = stage.tile([P, PASSES, N_BLOCK], U32, align_bytes=64, name="w_codes")
+                    w_scales[cb] = stage.tile([P, PASSES, N_BLOCK], U8, align_bytes=64, name="w_scales")
                 cols = slice(i * P, (i + 1) * P)
                 for g in range(PASSES):
                     nc.vector.quantize_mx(
                         out=w_codes[cb][:, g, cols].bitcast(E4M3_X4),
                         scales=w_scales[cb][:, g, cols],
-                        in_=w_grouped[:, g, :],
+                        in_=w_grouped[before][:, g, :],
                     )
-            if cb >= 1:
-                done, tt = cb - 1, i
+            if 0 <= before < TOKEN_TILES:
+                for b in range(PASSES // 2):
+                    two = slice(2 * b, 2 * b + 2)
+                    nc.vector.quantize_mx(
+                        out=gq_codes[:, before, two, :].rearrange("p g r -> p (g r)").bitcast(E5M2_X4),
+                        scales=gq_scales[:, before, two, :].rearrange("p g r -> p (g r)"),
+                        in_=gq_grouped[before][:, two, :].rearrange("p g e -> p (g e)"),
+                    )
+
+            product = r - (C_TILES_PER_BLOCK - 1) - PRODUCT_LAG
+            if 0 <= product < PRODUCTS:
+                cb, tt = divmod(product, TOKEN_TILES)
                 acc = sums.tile([P, N_BLOCK], F32)
                 for g in range(PASSES):
                     nc.tensor.matmul_mx(
                         out=acc[:],
                         lhsT=gq_codes[:, tt, g, :].bitcast(E5M2_X4),
                         lhsT_scale=gq_scales[:, tt, g, :],
-                        rhs=w_codes[done][:, g, :].bitcast(E4M3_X4),
-                        rhs_scale=w_scales[done][:, g, :],
+                        rhs=w_codes[cb][:, g, :].bitcast(E4M3_X4),
+                        rhs_scale=w_scales[cb][:, g, :],
                         start=(g == 0),
                         stop=(g == PASSES - 1),
                     )
                 result = stage.tile([P, N_BLOCK], F32)
                 nc.scalar.copy(out=result[:], in_=acc[:])
                 nc.sync.dma_start(
-                    out=out_dram[tt * P : (tt + 1) * P, done * N_BLOCK : (done + 1) * N_BLOCK], in_=result[:]
+                    out=out_dram[tt * P : (tt + 1) * P, cb * N_BLOCK : (cb + 1) * N_BLOCK], in_=result[:]
                 )

@@ -27,7 +27,8 @@ C_TILES = C // P
 C_TILES_PER_BLOCK = N_BLOCK // P
 PRODUCTS = TOKEN_TILES * (C // N_BLOCK)
 
-PRODUCT_LAG = 2
+ROUNDS_PER_TOKEN_TILE = 2
+FIRST_PRODUCT_ROUND = C_TILES_PER_BLOCK
 UNSORTED_TILES = 6
 
 FLOPS = 2 * TOKENS * C * K
@@ -45,6 +46,11 @@ def undo_rotation(nc, work, rows, cos, sin):
     nc.vector.tensor_mul(out=by_sin[:], in0=rotated, in1=sin.unsqueeze(1).unsqueeze(1).to_broadcast(shape))
     nc.vector.tensor_add(out=rotated[:, :, 0, :], in0=by_cos[:, :, 0, :], in1=by_sin[:, :, 1, :])
     nc.vector.tensor_sub(out=rotated[:, :, 1, :], in0=by_cos[:, :, 1, :], in1=by_sin[:, :, 0, :])
+
+
+def token_tile_of_round(r):
+    tt, rest = divmod(r, ROUNDS_PER_TOKEN_TILE)
+    return tt if rest == 0 and 0 <= tt < TOKEN_TILES else None
 
 
 def k_onto_partitions(nc, banks, identity, words, grouped):
@@ -73,12 +79,18 @@ def tile_fa3mlaattention_pb_kernel(tc, x, freqs_cis, w_q, grad_out, out):
 
         freqs = keep.tile([P, POSITIONS // P, NF, 2], BF16)
         nc.sync.dma_start(out=freqs[:], in_=freqs_cis.rearrange("(a p) j s -> p a j s", p=P))
-        g_rows = keep.tile([P, TOKEN_TILES, K], BF16)
-        w_rows = keep.tile([P, C_TILES, K], BF16)
-        for r in range(C_TILES):
-            if r < TOKEN_TILES:
-                nc.sync.dma_start(out=g_rows[:, r, :], in_=g_dram[r * P : (r + 1) * P, :])
-            nc.sync.dma_start(out=w_rows[:, r, :], in_=w_q[r * P : (r + 1) * P, :])
+        g_rows = keep.tile([P, TOKEN_TILES, PASSES, K_PASS], BF16, align_bytes=64)
+        w_rows = keep.tile([P, C_TILES, PASSES, K_PASS], BF16, align_bytes=64)
+        for r in range(-1, C_TILES):
+            tt = token_tile_of_round(r + 1)
+            if tt is not None:
+                nc.sync.dma_start(
+                    out=g_rows[:, tt, :, :].rearrange("p g e -> p (g e)"), in_=g_dram[tt * P : (tt + 1) * P, :]
+                )
+            if r >= 0:
+                nc.sync.dma_start(
+                    out=w_rows[:, r, :, :].rearrange("p g e -> p (g e)"), in_=w_q[r * P : (r + 1) * P, :]
+                )
 
         identity = keep.tile([P, P], F32)
         make_identity(nc, identity[:])
@@ -88,35 +100,33 @@ def tile_fa3mlaattention_pb_kernel(tc, x, freqs_cis, w_q, grad_out, out):
         w_codes = {}
         w_scales = {}
         w_words = {}
-        w_grouped = {}
-        gq_grouped = {}
 
-        for r in range(C_TILES + PRODUCT_LAG + C_TILES_PER_BLOCK - 1):
-            if r < TOKEN_TILES:
-                a = r % (POSITIONS // P)
-                undo_rotation(nc, keep, g_rows[:, r, :], freqs[:, a, :, 0], freqs[:, a, :, 1])
-
-            ahead = r + 1
-            if UNSORTED_TILES <= ahead < C_TILES:
+        for r in range(-1, FIRST_PRODUCT_ROUND + PRODUCTS):
+            tt = token_tile_of_round(r + 1)
+            if tt is not None:
+                a = tt % (POSITIONS // P)
+                undo_rotation(
+                    nc, keep, g_rows[:, tt, :, :].rearrange("p g e -> p (g e)"), freqs[:, a, :, 0], freqs[:, a, :, 1]
+                )
+            if UNSORTED_TILES <= r + 1 < C_TILES:
                 w_sorted = stage.tile([P, 2, K // 4], F32)
                 nc.vector.tensor_copy(
-                    out=w_sorted[:], in_=w_rows[:, ahead, :].bitcast(F32).rearrange("p (w u) -> p u w", u=2)
+                    out=w_sorted[:],
+                    in_=w_rows[:, r + 1, :, :].rearrange("p g e -> p (g e)").bitcast(F32).rearrange("p (w u) -> p u w", u=2),
                 )
-                w_words[ahead] = w_sorted[:].rearrange("p u (g w) -> p g u w", g=PASSES)
+                w_words[r + 1] = w_sorted[:].rearrange("p u (g w) -> p g u w", g=PASSES)
 
-            if r < C_TILES:
+            if 0 <= r < C_TILES:
                 if r < UNSORTED_TILES:
-                    w_words[r] = w_rows[:, r, :].bitcast(F32).rearrange("p (g w u) -> p g u w", g=PASSES, u=2)
-                w_grouped[r] = stage.tile([P, PASSES, 4 * P], BF16, align_bytes=64, name="w_grouped")
-                k_onto_partitions(nc, banks, identity[:], w_words[r], w_grouped[r][:])
-            if r < TOKEN_TILES:
-                gq_words = g_rows[:, r, :].bitcast(F32).rearrange("p (g w u) -> p g u w", g=PASSES, u=2)
-                gq_grouped[r] = stage.tile([P, PASSES, 4 * P], BF16, align_bytes=64, name="gq_grouped")
-                k_onto_partitions(nc, banks, identity[:], gq_words, gq_grouped[r][:])
+                    w_words[r] = w_rows[:, r, :, :].bitcast(F32).rearrange("p g (w u) -> p g u w", u=2)
+                k_onto_partitions(nc, banks, identity[:], w_words[r], w_rows[:, r, :, :])
+            tt = token_tile_of_round(r)
+            if tt is not None:
+                gq_words = g_rows[:, tt, :, :].bitcast(F32).rearrange("p g (w u) -> p g u w", u=2)
+                k_onto_partitions(nc, banks, identity[:], gq_words, g_rows[:, tt, :, :])
 
-            before = r - 1
-            if 0 <= before < C_TILES:
-                cb, i = divmod(before, C_TILES_PER_BLOCK)
+            if 0 <= r - 1 < C_TILES:
+                cb, i = divmod(r - 1, C_TILES_PER_BLOCK)
                 if i == 0:
                     w_codes[cb] = stage.tile([P, PASSES, N_BLOCK], U32, align_bytes=64, name="w_codes")
                     w_scales[cb] = stage.tile([P, PASSES, N_BLOCK], U8, align_bytes=64, name="w_scales")
@@ -125,20 +135,20 @@ def tile_fa3mlaattention_pb_kernel(tc, x, freqs_cis, w_q, grad_out, out):
                     nc.vector.quantize_mx(
                         out=w_codes[cb][:, g, cols].bitcast(E4M3_X4),
                         scales=w_scales[cb][:, g, cols],
-                        in_=w_grouped[before][:, g, :],
+                        in_=w_rows[:, r - 1, g, :],
                     )
-            if 0 <= before < TOKEN_TILES:
+            tt = token_tile_of_round(r - 1)
+            if tt is not None:
                 for b in range(PASSES // 2):
                     two = slice(2 * b, 2 * b + 2)
                     nc.vector.quantize_mx(
-                        out=gq_codes[:, before, two, :].rearrange("p g r -> p (g r)").bitcast(E5M2_X4),
-                        scales=gq_scales[:, before, two, :].rearrange("p g r -> p (g r)"),
-                        in_=gq_grouped[before][:, two, :].rearrange("p g e -> p (g e)"),
+                        out=gq_codes[:, tt, two, :].rearrange("p g r -> p (g r)").bitcast(E5M2_X4),
+                        scales=gq_scales[:, tt, two, :].rearrange("p g r -> p (g r)"),
+                        in_=g_rows[:, tt, two, :].rearrange("p g e -> p (g e)"),
                     )
 
-            product = r - (C_TILES_PER_BLOCK - 1) - PRODUCT_LAG
-            if 0 <= product < PRODUCTS:
-                cb, tt = divmod(product, TOKEN_TILES)
+            if r >= FIRST_PRODUCT_ROUND:
+                cb, tt = divmod(r - FIRST_PRODUCT_ROUND, TOKEN_TILES)
                 acc = sums.tile([P, N_BLOCK], F32)
                 for g in range(PASSES):
                     nc.tensor.matmul_mx(

@@ -27,8 +27,7 @@ C_TILES = C // P
 C_TILES_PER_BLOCK = N_BLOCK // P
 PRODUCTS = TOKEN_TILES * (C // N_BLOCK)
 
-ROUNDS_PER_TOKEN_TILE = 2
-FIRST_PRODUCT_ROUND = C_TILES_PER_BLOCK
+PRODUCT_LAG = 2
 UNSORTED_TILES = 6
 
 FLOPS = 2 * TOKENS * C * K
@@ -46,11 +45,6 @@ def undo_rotation(nc, work, rows, cos, sin):
     nc.vector.tensor_mul(out=by_sin[:], in0=rotated, in1=sin.unsqueeze(1).unsqueeze(1).to_broadcast(shape))
     nc.vector.tensor_add(out=rotated[:, :, 0, :], in0=by_cos[:, :, 0, :], in1=by_sin[:, :, 1, :])
     nc.vector.tensor_sub(out=rotated[:, :, 1, :], in0=by_cos[:, :, 1, :], in1=by_sin[:, :, 0, :])
-
-
-def token_tile_of_round(r):
-    tt, rest = divmod(r, ROUNDS_PER_TOKEN_TILE)
-    return tt if rest == 0 and 0 <= tt < TOKEN_TILES else None
 
 
 def k_onto_partitions(nc, banks, identity, words, grouped):
@@ -79,18 +73,12 @@ def tile_fa3mlaattention_pb_kernel(tc, x, freqs_cis, w_q, grad_out, out):
 
         freqs = keep.tile([P, POSITIONS // P, NF, 2], BF16)
         nc.sync.dma_start(out=freqs[:], in_=freqs_cis.rearrange("(a p) j s -> p a j s", p=P))
-        g_rows = keep.tile([P, TOKEN_TILES, PASSES, K_PASS], BF16, align_bytes=64)
-        w_rows = keep.tile([P, C_TILES, PASSES, K_PASS], BF16, align_bytes=64)
-        for r in range(-1, C_TILES):
-            tt = token_tile_of_round(r + 1)
-            if tt is not None:
-                nc.sync.dma_start(
-                    out=g_rows[:, tt, :, :].rearrange("p g e -> p (g e)"), in_=g_dram[tt * P : (tt + 1) * P, :]
-                )
-            if r >= 0:
-                nc.sync.dma_start(
-                    out=w_rows[:, r, :, :].rearrange("p g e -> p (g e)"), in_=w_q[r * P : (r + 1) * P, :]
-                )
+        g_rows = keep.tile([P, TOKEN_TILES, K], BF16)
+        w_rows = keep.tile([P, C_TILES, K], BF16)
+        for r in range(C_TILES):
+            if r < TOKEN_TILES:
+                nc.sync.dma_start(out=g_rows[:, r, :], in_=g_dram[r * P : (r + 1) * P, :])
+            nc.sync.dma_start(out=w_rows[:, r, :], in_=w_q[r * P : (r + 1) * P, :])
 
         identity = keep.tile([P, P], F32)
         make_identity(nc, identity[:])
@@ -100,33 +88,35 @@ def tile_fa3mlaattention_pb_kernel(tc, x, freqs_cis, w_q, grad_out, out):
         w_codes = {}
         w_scales = {}
         w_words = {}
+        w_grouped = {}
+        gq_grouped = {}
 
-        for r in range(-1, FIRST_PRODUCT_ROUND + PRODUCTS):
-            tt = token_tile_of_round(r + 1)
-            if tt is not None:
-                a = tt % (POSITIONS // P)
-                undo_rotation(
-                    nc, keep, g_rows[:, tt, :, :].rearrange("p g e -> p (g e)"), freqs[:, a, :, 0], freqs[:, a, :, 1]
-                )
-            if UNSORTED_TILES <= r + 1 < C_TILES:
+        for r in range(C_TILES + PRODUCT_LAG + C_TILES_PER_BLOCK - 1):
+            if r < TOKEN_TILES:
+                a = r % (POSITIONS // P)
+                undo_rotation(nc, keep, g_rows[:, r, :], freqs[:, a, :, 0], freqs[:, a, :, 1])
+
+            ahead = r + 1
+            if UNSORTED_TILES <= ahead < C_TILES:
                 w_sorted = stage.tile([P, 2, K // 4], F32)
                 nc.vector.tensor_copy(
-                    out=w_sorted[:],
-                    in_=w_rows[:, r + 1, :, :].rearrange("p g e -> p (g e)").bitcast(F32).rearrange("p (w u) -> p u w", u=2),
+                    out=w_sorted[:], in_=w_rows[:, ahead, :].bitcast(F32).rearrange("p (w u) -> p u w", u=2)
                 )
-                w_words[r + 1] = w_sorted[:].rearrange("p u (g w) -> p g u w", g=PASSES)
+                w_words[ahead] = w_sorted[:].rearrange("p u (g w) -> p g u w", g=PASSES)
 
-            if 0 <= r < C_TILES:
+            if r < C_TILES:
                 if r < UNSORTED_TILES:
-                    w_words[r] = w_rows[:, r, :, :].bitcast(F32).rearrange("p g (w u) -> p g u w", u=2)
-                k_onto_partitions(nc, banks, identity[:], w_words[r], w_rows[:, r, :, :])
-            tt = token_tile_of_round(r)
-            if tt is not None:
-                gq_words = g_rows[:, tt, :, :].bitcast(F32).rearrange("p g (w u) -> p g u w", u=2)
-                k_onto_partitions(nc, banks, identity[:], gq_words, g_rows[:, tt, :, :])
+                    w_words[r] = w_rows[:, r, :].bitcast(F32).rearrange("p (g w u) -> p g u w", g=PASSES, u=2)
+                w_grouped[r] = stage.tile([P, PASSES, 4 * P], BF16, align_bytes=64, name="w_grouped")
+                k_onto_partitions(nc, banks, identity[:], w_words[r], w_grouped[r][:])
+            before = r - 1
+            if 0 <= before < TOKEN_TILES:
+                gq_words = g_rows[:, before, :].bitcast(F32).rearrange("p (g w u) -> p g u w", g=PASSES, u=2)
+                gq_grouped[before] = stage.tile([P, PASSES, 4 * P], BF16, align_bytes=64, name="gq_grouped")
+                k_onto_partitions(nc, banks, identity[:], gq_words, gq_grouped[before][:])
 
-            if 0 <= r - 1 < C_TILES:
-                cb, i = divmod(r - 1, C_TILES_PER_BLOCK)
+            if 0 <= before < C_TILES:
+                cb, i = divmod(before, C_TILES_PER_BLOCK)
                 if i == 0:
                     w_codes[cb] = stage.tile([P, PASSES, N_BLOCK], U32, align_bytes=64, name="w_codes")
                     w_scales[cb] = stage.tile([P, PASSES, N_BLOCK], U8, align_bytes=64, name="w_scales")
@@ -135,20 +125,21 @@ def tile_fa3mlaattention_pb_kernel(tc, x, freqs_cis, w_q, grad_out, out):
                     nc.vector.quantize_mx(
                         out=w_codes[cb][:, g, cols].bitcast(E4M3_X4),
                         scales=w_scales[cb][:, g, cols],
-                        in_=w_rows[:, r - 1, g, :],
+                        in_=w_grouped[before][:, g, :],
                     )
-            tt = token_tile_of_round(r - 1)
-            if tt is not None:
+            tt = r - 2
+            if 0 <= tt < TOKEN_TILES:
                 for b in range(PASSES // 2):
                     two = slice(2 * b, 2 * b + 2)
                     nc.vector.quantize_mx(
                         out=gq_codes[:, tt, two, :].rearrange("p g r -> p (g r)").bitcast(E5M2_X4),
                         scales=gq_scales[:, tt, two, :].rearrange("p g r -> p (g r)"),
-                        in_=g_rows[:, tt, two, :].rearrange("p g e -> p (g e)"),
+                        in_=gq_grouped[tt][:, two, :].rearrange("p g e -> p (g e)"),
                     )
 
-            if r >= FIRST_PRODUCT_ROUND:
-                cb, tt = divmod(r - FIRST_PRODUCT_ROUND, TOKEN_TILES)
+            product = r - (C_TILES_PER_BLOCK - 1) - PRODUCT_LAG
+            if 0 <= product < PRODUCTS:
+                cb, tt = divmod(product, TOKEN_TILES)
                 acc = sums.tile([P, N_BLOCK], F32)
                 for g in range(PASSES):
                     nc.tensor.matmul_mx(

@@ -25,38 +25,18 @@ N_BLOCK = 512
 TOKEN_TILES = TOKENS // P
 C_TILES = C // P
 C_TILES_PER_BLOCK = N_BLOCK // P
-PRODUCTS = TOKEN_TILES * (C // N_BLOCK)
-
-PRODUCT_LAG = 2
-UNSORTED_TILES = 6
+C_BLOCKS = C // N_BLOCK
 
 FLOPS = 2 * TOKENS * C * K
 BYTES = 2 * C * K + 2 * TOKENS * K + 2 * POSITIONS * NF * 2 + 4 * TOKENS * C
 
-
-def undo_rotation(nc, work, rows, cos, sin):
-    shape = [P, HEADS, 2, NF]
-    rotated = rows.rearrange("p (h d) -> p h d", d=HEAD)[:, :, PLAIN:HEAD].rearrange(
-        "p h (f j) -> p h f j", f=2
-    )
-    by_cos = work.tile(shape, F32)
-    by_sin = work.tile(shape, F32)
-    nc.vector.tensor_mul(out=by_cos[:], in0=rotated, in1=cos.unsqueeze(1).unsqueeze(1).to_broadcast(shape))
-    nc.vector.tensor_mul(out=by_sin[:], in0=rotated, in1=sin.unsqueeze(1).unsqueeze(1).to_broadcast(shape))
-    nc.vector.tensor_add(out=rotated[:, :, 0, :], in0=by_cos[:, :, 0, :], in1=by_sin[:, :, 1, :])
-    nc.vector.tensor_sub(out=rotated[:, :, 1, :], in0=by_cos[:, :, 1, :], in1=by_sin[:, :, 0, :])
-
-
-def k_onto_partitions(nc, banks, identity, words, grouped):
-    grouped_words = grouped.bitcast(F32).rearrange("p g (r u) -> p g r u", u=2)
-    for b in range(PASSES // 2):
-        bank = banks.tile([P, 2, 2, P], F32)
-        for g in range(2):
-            for u in range(2):
-                nc.tensor.transpose(bank[:, g, u, :], words[:, 2 * b + g, u, :], identity)
-        nc.scalar.copy(
-            out=grouped_words[:, 2 * b : 2 * b + 2, :, :], in_=bank[:].rearrange("p g u r -> p g r u")
-        )
+LOADS = "g0 w0 w1 g1 w2 w3 w4 w5 g2 g3 w6 w7 w8 w9 w10 w11 w12 w13 w14 w15"
+SCRIPT = "T:w0 T:w1 R:0c R:0s R:0a T:g0 Q:w0 T:w2 R:1c Q:w1 T:w3 R:1s Q:g0 R:1a T:g1 Q:w2 T:w4 Q:w3 T:w5 P:00 Q:g1 P:01 T:w6 R:2c Q:w4 T:w7 R:2s R:3c Q:w5 R:2a T:g2 R:3s Q:w6 R:3a T:g3 Q:w7 P:10 P:11 S:w8 T:w8 Q:g2 S:w9 T:w9 P:02 P:12 Q:g3 S:w10 T:w10 Q:w8 S:w11 T:w11 P:03 P:13 Q:w9 S:w12 T:w12 Q:w10 S:w13 T:w13 Q:w11 P:20 P:21 S:w14 T:w14 Q:w12 S:w15 T:w15 P:22 P:23 Q:w13 Q:w14 Q:w15 P:30 P:31 P:32 P:33"
+W_CODE_BUFS = 3
+GROUPED_BUFS = 3
+SORTED_BUFS = 2
+T_BANKS = 6
+RESULT_BUFS = 4
 
 
 def tile_fa3mlaattention_pb_kernel(tc, x, freqs_cis, w_q, grad_out, out):
@@ -68,17 +48,22 @@ def tile_fa3mlaattention_pb_kernel(tc, x, freqs_cis, w_q, grad_out, out):
         ctx.enter_context(tc.manual_schedule())
         keep = ctx.enter_context(tc.tile_pool(name="keep", bufs=1))
         stage = ctx.enter_context(tc.tile_pool(name="stage", bufs=2))
-        banks = ctx.enter_context(tc.psum_pool(name="banks", bufs=6))
-        sums = ctx.enter_context(tc.psum_pool(name="sums", bufs=2))
+        banks = ctx.enter_context(tc.psum_pool(name="banks", bufs=T_BANKS))
+        sums = ctx.enter_context(tc.psum_pool(name="sums", bufs=8 - T_BANKS))
 
         freqs = keep.tile([P, POSITIONS // P, NF, 2], BF16)
         nc.sync.dma_start(out=freqs[:], in_=freqs_cis.rearrange("(a p) j s -> p a j s", p=P))
         g_rows = keep.tile([P, TOKEN_TILES, K], BF16)
         w_rows = keep.tile([P, C_TILES, K], BF16)
-        for r in range(C_TILES):
-            if r < TOKEN_TILES:
-                nc.sync.dma_start(out=g_rows[:, r, :], in_=g_dram[r * P : (r + 1) * P, :])
-            nc.sync.dma_start(out=w_rows[:, r, :], in_=w_q[r * P : (r + 1) * P, :])
+        rows = {}
+        for t in LOADS.split():
+            i = int(t[1:])
+            if t[0] == "g":
+                nc.sync.dma_start(out=g_rows[:, i, :], in_=g_dram[i * P : (i + 1) * P, :])
+                rows[t] = g_rows[:, i, :]
+            else:
+                nc.sync.dma_start(out=w_rows[:, i, :], in_=w_q[i * P : (i + 1) * P, :])
+                rows[t] = w_rows[:, i, :]
 
         identity = keep.tile([P, P], F32)
         make_identity(nc, identity[:])
@@ -87,72 +72,111 @@ def tile_fa3mlaattention_pb_kernel(tc, x, freqs_cis, w_q, grad_out, out):
         gq_scales = keep.tile([P, TOKEN_TILES, PASSES, P], U8, align_bytes=64)
         w_codes = {}
         w_scales = {}
-        w_words = {}
-        w_grouped = {}
-        gq_grouped = {}
+        words = {}
+        grouped = {}
+        partial = {}
+        shape = [P, HEADS, 2, NF]
 
-        for r in range(C_TILES + PRODUCT_LAG + C_TILES_PER_BLOCK - 1):
-            if r < TOKEN_TILES:
-                a = r % (POSITIONS // P)
-                undo_rotation(nc, keep, g_rows[:, r, :], freqs[:, a, :, 0], freqs[:, a, :, 1])
+        def rotated_of(tt):
+            return g_rows[:, tt, :].rearrange("p (h d) -> p h d", d=HEAD)[:, :, PLAIN:HEAD].rearrange(
+                "p h (f j) -> p h f j", f=2
+            )
 
-            ahead = r + 1
-            if UNSORTED_TILES <= ahead < C_TILES:
-                w_sorted = stage.tile([P, 2, K // 4], F32)
-                nc.vector.tensor_copy(
-                    out=w_sorted[:], in_=w_rows[:, ahead, :].bitcast(F32).rearrange("p (w u) -> p u w", u=2)
-                )
-                w_words[ahead] = w_sorted[:].rearrange("p u (g w) -> p g u w", g=PASSES)
+        def rotate_step(tt, step):
+            a = tt % (POSITIONS // P)
+            rotated = rotated_of(tt)
+            if step == "c":
+                by_cos = stage.tile(shape, F32, name="by_cos", bufs=2)
+                cos = freqs[:, a, :, 0].unsqueeze(1).unsqueeze(1).to_broadcast(shape)
+                nc.vector.tensor_mul(out=by_cos[:], in0=rotated, in1=cos)
+                partial[(tt, 0)] = by_cos
+            if step == "s":
+                by_sin = stage.tile(shape, F32, name="by_sin", bufs=2)
+                sin = freqs[:, a, :, 1].unsqueeze(1).unsqueeze(1).to_broadcast(shape)
+                nc.vector.tensor_mul(out=by_sin[:], in0=rotated, in1=sin)
+                partial[(tt, 1)] = by_sin
+            if step == "a":
+                by_cos, by_sin = partial[(tt, 0)], partial[(tt, 1)]
+                nc.vector.tensor_add(out=rotated[:, :, 0, :], in0=by_cos[:, :, 0, :], in1=by_sin[:, :, 1, :])
+                nc.vector.tensor_sub(out=rotated[:, :, 1, :], in0=by_cos[:, :, 1, :], in1=by_sin[:, :, 0, :])
 
-            if r < C_TILES:
-                if r < UNSORTED_TILES:
-                    w_words[r] = w_rows[:, r, :].bitcast(F32).rearrange("p (g w u) -> p g u w", g=PASSES, u=2)
-                w_grouped[r] = stage.tile([P, PASSES, 4 * P], BF16, align_bytes=64, name="w_grouped")
-                k_onto_partitions(nc, banks, identity[:], w_words[r], w_grouped[r][:])
-            before = r - 1
-            if 0 <= before < TOKEN_TILES:
-                gq_words = g_rows[:, before, :].bitcast(F32).rearrange("p (g w u) -> p g u w", g=PASSES, u=2)
-                gq_grouped[before] = stage.tile([P, PASSES, 4 * P], BF16, align_bytes=64, name="gq_grouped")
-                k_onto_partitions(nc, banks, identity[:], gq_words, gq_grouped[before][:])
+        def sort_words(t, engine):
+            w_sorted = stage.tile([P, 2, K // 4], F32, name="w_sorted", bufs=SORTED_BUFS)
+            src = rows[t].bitcast(F32).rearrange("p (w u) -> p u w", u=2)
+            if engine == "D":
+                nc.vector.tensor_copy(out=w_sorted[:], in_=src)
+            else:
+                nc.scalar.copy(out=w_sorted[:], in_=src)
+            words[t] = w_sorted[:].rearrange("p u (g w) -> p g u w", g=PASSES)
 
-            if 0 <= before < C_TILES:
-                cb, i = divmod(before, C_TILES_PER_BLOCK)
-                if i == 0:
-                    w_codes[cb] = stage.tile([P, PASSES, N_BLOCK], U32, align_bytes=64, name="w_codes")
-                    w_scales[cb] = stage.tile([P, PASSES, N_BLOCK], U8, align_bytes=64, name="w_scales")
-                cols = slice(i * P, (i + 1) * P)
+        def transpose(t, engines):
+            if t not in words:
+                words[t] = rows[t].bitcast(F32).rearrange("p (g w u) -> p g u w", g=PASSES, u=2)
+            grouped[t] = stage.tile([P, PASSES, 4 * P], BF16, align_bytes=64, name="grouped", bufs=GROUPED_BUFS)
+            grouped_words = grouped[t][:].bitcast(F32).rearrange("p g (r u) -> p g r u", u=2)
+            for b in range(PASSES // 2):
+                bank = banks.tile([P, 2, 2, P], F32)
+                for g in range(2):
+                    for u in range(2):
+                        nc.tensor.transpose(bank[:, g, u, :], words[t][:, 2 * b + g, u, :], identity[:])
+                dst = grouped_words[:, 2 * b : 2 * b + 2, :, :]
+                src = bank[:].rearrange("p g u r -> p g r u")
+                if engines[b] == "D":
+                    nc.vector.tensor_copy(out=dst, in_=src)
+                else:
+                    nc.scalar.copy(out=dst, in_=src)
+
+        def quantise(t):
+            i = int(t[1:])
+            if t[0] == "w":
+                cb, j = divmod(i, C_TILES_PER_BLOCK)
+                if cb not in w_codes:
+                    w_codes[cb] = stage.tile([P, PASSES, N_BLOCK], U32, align_bytes=64, name="w_codes", bufs=W_CODE_BUFS)
+                    w_scales[cb] = stage.tile([P, PASSES, N_BLOCK], U8, align_bytes=64, name="w_scales", bufs=W_CODE_BUFS)
+                cols = slice(j * P, (j + 1) * P)
                 for g in range(PASSES):
                     nc.vector.quantize_mx(
                         out=w_codes[cb][:, g, cols].bitcast(E4M3_X4),
                         scales=w_scales[cb][:, g, cols],
-                        in_=w_grouped[before][:, g, :],
+                        in_=grouped[t][:, g, :],
                     )
-            tt = r - 2
-            if 0 <= tt < TOKEN_TILES:
+            else:
                 for b in range(PASSES // 2):
                     two = slice(2 * b, 2 * b + 2)
                     nc.vector.quantize_mx(
-                        out=gq_codes[:, tt, two, :].rearrange("p g r -> p (g r)").bitcast(E5M2_X4),
-                        scales=gq_scales[:, tt, two, :].rearrange("p g r -> p (g r)"),
-                        in_=gq_grouped[tt][:, two, :].rearrange("p g e -> p (g e)"),
+                        out=gq_codes[:, i, two, :].rearrange("p g r -> p (g r)").bitcast(E5M2_X4),
+                        scales=gq_scales[:, i, two, :].rearrange("p g r -> p (g r)"),
+                        in_=grouped[t][:, two, :].rearrange("p g e -> p (g e)"),
                     )
 
-            product = r - (C_TILES_PER_BLOCK - 1) - PRODUCT_LAG
-            if 0 <= product < PRODUCTS:
-                cb, tt = divmod(product, TOKEN_TILES)
-                acc = sums.tile([P, N_BLOCK], F32)
-                for g in range(PASSES):
-                    nc.tensor.matmul_mx(
-                        out=acc[:],
-                        lhsT=gq_codes[:, tt, g, :].bitcast(E5M2_X4),
-                        lhsT_scale=gq_scales[:, tt, g, :],
-                        rhs=w_codes[cb][:, g, :].bitcast(E4M3_X4),
-                        rhs_scale=w_scales[cb][:, g, :],
-                        start=(g == 0),
-                        stop=(g == PASSES - 1),
-                    )
-                result = stage.tile([P, N_BLOCK], F32)
-                nc.scalar.copy(out=result[:], in_=acc[:])
-                nc.sync.dma_start(
-                    out=out_dram[tt * P : (tt + 1) * P, cb * N_BLOCK : (cb + 1) * N_BLOCK], in_=result[:]
+        def product(cb, tt, engine):
+            acc = sums.tile([P, N_BLOCK], F32)
+            for g in range(PASSES):
+                nc.tensor.matmul_mx(
+                    out=acc[:],
+                    lhsT=gq_codes[:, tt, g, :].bitcast(E5M2_X4),
+                    lhsT_scale=gq_scales[:, tt, g, :],
+                    rhs=w_codes[cb][:, g, :].bitcast(E4M3_X4),
+                    rhs_scale=w_scales[cb][:, g, :],
+                    start=(g == 0),
+                    stop=(g == PASSES - 1),
                 )
+            result = stage.tile([P, N_BLOCK], F32, name="result", bufs=RESULT_BUFS)
+            if engine == "D":
+                nc.vector.tensor_copy(out=result[:], in_=acc[:])
+            else:
+                nc.scalar.copy(out=result[:], in_=acc[:])
+            nc.sync.dma_start(out=out_dram[tt * P : (tt + 1) * P, cb * N_BLOCK : (cb + 1) * N_BLOCK], in_=result[:])
+
+        for tok in SCRIPT.split():
+            f = tok.split(":")
+            if f[0] == "R":
+                rotate_step(int(f[1][0]), f[1][1])
+            elif f[0] == "S":
+                sort_words(f[1], f[2] if len(f) > 2 else "D")
+            elif f[0] == "T":
+                transpose(f[1], f[2] if len(f) > 2 else "AAA")
+            elif f[0] == "Q":
+                quantise(f[1])
+            elif f[0] == "P":
+                product(int(f[1][0]), int(f[1][1]), f[2] if len(f) > 2 else "A")

@@ -34,9 +34,11 @@ LOADS = "g0 w0 w1 g1 w2 w3 w4 w5 g2 g3 w6 w7 w8 w9 w10 w11 w12 w13 w14 w15"
 SCRIPT = "T:w0 T:w1 R:0c R:0s R:0a T:g0 Q:w0 T:w2 R:1c Q:w1 T:w3 R:1s Q:g0 R:1a T:g1 Q:w2 T:w4 Q:w3 T:w5 P:00 Q:g1 P:01 T:w6 R:2c Q:w4 T:w7 R:2s R:3c Q:w5 R:2a T:g2 R:3s Q:w6 R:3a T:g3 Q:w7 P:10 P:11 S:w8 T:w8 Q:g2 S:w9 T:w9 P:02 P:12 Q:g3 S:w10 T:w10 Q:w8 S:w11 T:w11 P:03 P:13 Q:w9 S:w12 T:w12 Q:w10 S:w13 T:w13 Q:w11 P:20 P:21 S:w14 T:w14 Q:w12 S:w15 T:w15 P:22 P:23 Q:w13 Q:w14 Q:w15 P:30 P:31 P:32 P:33"
 W_CODE_BUFS = 3
 GROUPED_BUFS = 3
-SORTED_BUFS = 2
 T_BANKS = 6
-RESULT_BUFS = 4
+RESULT_BUFS = 8
+ROT_BUFS = 2
+PAIRS = False
+PAIR_BUFS = 2
 
 
 def tile_fa3mlaattention_pb_kernel(tc, x, freqs_cis, w_q, grad_out, out):
@@ -54,16 +56,17 @@ def tile_fa3mlaattention_pb_kernel(tc, x, freqs_cis, w_q, grad_out, out):
         freqs = keep.tile([P, POSITIONS // P, NF, 2], BF16)
         nc.sync.dma_start(out=freqs[:], in_=freqs_cis.rearrange("(a p) j s -> p a j s", p=P))
         g_rows = keep.tile([P, TOKEN_TILES, K], BF16)
-        w_rows = keep.tile([P, C_TILES, K], BF16)
         rows = {}
         for t in LOADS.split():
-            i = int(t[1:])
+            i = int(t[1:3]) if t[0] == "w" else int(t[1])
             if t[0] == "g":
-                nc.sync.dma_start(out=g_rows[:, i, :], in_=g_dram[i * P : (i + 1) * P, :])
-                rows[t] = g_rows[:, i, :]
+                cols = {"": slice(0, K), "A": slice(0, K // 2), "B": slice(K // 2, K)}[t[2:]]
+                nc.sync.dma_start(out=g_rows[:, i, cols], in_=g_dram[i * P : (i + 1) * P, cols])
+                rows[t[:2]] = g_rows[:, i, :]
             else:
-                nc.sync.dma_start(out=w_rows[:, i, :], in_=w_q[i * P : (i + 1) * P, :])
-                rows[t] = w_rows[:, i, :]
+                w_rows = stage.tile([P, K], BF16, name="w_rows", bufs=C_TILES)
+                nc.sync.dma_start(out=w_rows[:], in_=w_q[i * P : (i + 1) * P, :])
+                rows[t] = w_rows[:]
 
         identity = keep.tile([P, P], F32)
         make_identity(nc, identity[:])
@@ -82,26 +85,28 @@ def tile_fa3mlaattention_pb_kernel(tc, x, freqs_cis, w_q, grad_out, out):
                 "p h (f j) -> p h f j", f=2
             )
 
-        def rotate_step(tt, step):
+        def rotate_step(tt, step, half):
             a = tt % (POSITIONS // P)
-            rotated = rotated_of(tt)
+            heads = {"": slice(0, HEADS), "A": slice(0, HEADS // 2), "B": slice(HEADS // 2, HEADS)}[half]
+            rotated = rotated_of(tt)[:, heads, :, :]
+            part = [P, HEADS if half == "" else HEADS // 2, 2, NF]
             if step == "c":
-                by_cos = stage.tile(shape, F32, name="by_cos", bufs=2)
-                cos = freqs[:, a, :, 0].unsqueeze(1).unsqueeze(1).to_broadcast(shape)
-                nc.vector.tensor_mul(out=by_cos[:], in0=rotated, in1=cos)
-                partial[(tt, 0)] = by_cos
+                if (tt, 0) not in partial:
+                    partial[(tt, 0)] = stage.tile(shape, F32, name="by_cos", bufs=ROT_BUFS)
+                cos = freqs[:, a, :, 0].unsqueeze(1).unsqueeze(1).to_broadcast(part)
+                nc.vector.tensor_mul(out=partial[(tt, 0)][:, heads, :, :], in0=rotated, in1=cos)
             if step == "s":
-                by_sin = stage.tile(shape, F32, name="by_sin", bufs=2)
-                sin = freqs[:, a, :, 1].unsqueeze(1).unsqueeze(1).to_broadcast(shape)
-                nc.vector.tensor_mul(out=by_sin[:], in0=rotated, in1=sin)
-                partial[(tt, 1)] = by_sin
+                if (tt, 1) not in partial:
+                    partial[(tt, 1)] = stage.tile(shape, F32, name="by_sin", bufs=ROT_BUFS)
+                sin = freqs[:, a, :, 1].unsqueeze(1).unsqueeze(1).to_broadcast(part)
+                nc.vector.tensor_mul(out=partial[(tt, 1)][:, heads, :, :], in0=rotated, in1=sin)
             if step == "a":
                 by_cos, by_sin = partial[(tt, 0)], partial[(tt, 1)]
-                nc.vector.tensor_add(out=rotated[:, :, 0, :], in0=by_cos[:, :, 0, :], in1=by_sin[:, :, 1, :])
-                nc.vector.tensor_sub(out=rotated[:, :, 1, :], in0=by_cos[:, :, 1, :], in1=by_sin[:, :, 0, :])
+                nc.vector.tensor_add(out=rotated[:, :, 0, :], in0=by_cos[:, heads, 0, :], in1=by_sin[:, heads, 1, :])
+                nc.vector.tensor_sub(out=rotated[:, :, 1, :], in0=by_cos[:, heads, 1, :], in1=by_sin[:, heads, 0, :])
 
         def sort_words(t, engine):
-            w_sorted = stage.tile([P, 2, K // 4], F32, name="w_sorted", bufs=SORTED_BUFS)
+            w_sorted = stage.tile([P, 2, K // 4], F32, name="w_rows", bufs=C_TILES)
             src = rows[t].bitcast(F32).rearrange("p (w u) -> p u w", u=2)
             if engine == "D":
                 nc.vector.tensor_copy(out=w_sorted[:], in_=src)
@@ -112,8 +117,15 @@ def tile_fa3mlaattention_pb_kernel(tc, x, freqs_cis, w_q, grad_out, out):
         def transpose(t, engines):
             if t not in words:
                 words[t] = rows[t].bitcast(F32).rearrange("p (g w u) -> p g u w", g=PASSES, u=2)
-            grouped[t] = stage.tile([P, PASSES, 4 * P], BF16, align_bytes=64, name="grouped", bufs=GROUPED_BUFS)
-            grouped_words = grouped[t][:].bitcast(F32).rearrange("p g (r u) -> p g r u", u=2)
+            if t[0] == "w" and PAIRS:
+                pair, j = divmod(int(t[1:]), 2)
+                if ("pair", pair) not in grouped:
+                    grouped[("pair", pair)] = stage.tile([P, PASSES, 2, 4 * P], BF16, align_bytes=64, name="grouped_pair", bufs=PAIR_BUFS)
+                grouped[t] = grouped[("pair", pair)][:, :, j, :]
+            else:
+                g_tile = stage.tile([P, PASSES, 4 * P], BF16, align_bytes=64, name="grouped", bufs=GROUPED_BUFS)
+                grouped[t] = g_tile[:]
+            grouped_words = grouped[t].bitcast(F32).rearrange("p g (r u) -> p g r u", u=2)
             for b in range(PASSES // 2):
                 bank = banks.tile([P, 2, 2, P], F32)
                 for g in range(2):
@@ -133,12 +145,13 @@ def tile_fa3mlaattention_pb_kernel(tc, x, freqs_cis, w_q, grad_out, out):
                 if cb not in w_codes:
                     w_codes[cb] = stage.tile([P, PASSES, N_BLOCK], U32, align_bytes=64, name="w_codes", bufs=W_CODE_BUFS)
                     w_scales[cb] = stage.tile([P, PASSES, N_BLOCK], U8, align_bytes=64, name="w_scales", bufs=W_CODE_BUFS)
-                cols = slice(j * P, (j + 1) * P)
+                n = 2 if PAIRS else 1
+                cols = slice(j * P, (j + n) * P)
                 for g in range(PASSES):
                     nc.vector.quantize_mx(
                         out=w_codes[cb][:, g, cols].bitcast(E4M3_X4),
                         scales=w_scales[cb][:, g, cols],
-                        in_=grouped[t][:, g, :],
+                        in_=grouped[("pair", i // 2)][:, g, :, :].rearrange("p j e -> p (j e)") if PAIRS else grouped[t][:, g, :],
                     )
             else:
                 for b in range(PASSES // 2):
@@ -162,16 +175,23 @@ def tile_fa3mlaattention_pb_kernel(tc, x, freqs_cis, w_q, grad_out, out):
                     stop=(g == PASSES - 1),
                 )
             result = stage.tile([P, N_BLOCK], F32, name="result", bufs=RESULT_BUFS)
-            if engine == "D":
-                nc.vector.tensor_copy(out=result[:], in_=acc[:])
-            else:
-                nc.scalar.copy(out=result[:], in_=acc[:])
-            nc.sync.dma_start(out=out_dram[tt * P : (tt + 1) * P, cb * N_BLOCK : (cb + 1) * N_BLOCK], in_=result[:])
+            pieces = 2 if engine == "H" else 1
+            width = N_BLOCK // pieces
+            for h in range(pieces):
+                cols = slice(h * width, (h + 1) * width)
+                if engine == "D":
+                    nc.vector.tensor_copy(out=result[:, cols], in_=acc[:, cols])
+                else:
+                    nc.scalar.copy(out=result[:, cols], in_=acc[:, cols])
+                nc.sync.dma_start(
+                    out=out_dram[tt * P : (tt + 1) * P, cb * N_BLOCK + h * width : cb * N_BLOCK + (h + 1) * width],
+                    in_=result[:, cols],
+                )
 
         for tok in SCRIPT.split():
             f = tok.split(":")
             if f[0] == "R":
-                rotate_step(int(f[1][0]), f[1][1])
+                rotate_step(int(f[1][0]), f[1][1], f[1][2:])
             elif f[0] == "S":
                 sort_words(f[1], f[2] if len(f) > 2 else "D")
             elif f[0] == "T":

from contextlib import ExitStack

import concourse.mybir as mybir
from concourse.masks import make_identity

F32 = mybir.dt.float32
BF16 = mybir.dt.bfloat16
U32 = mybir.dt.uint32
U8 = mybir.dt.uint8
E4M3_X4 = mybir.dt.float8_e4m3fn_x4
E5M2_X4 = mybir.dt.float8_e5m2_x4

P = 128
TOKENS = 512
POSITIONS = 256
HEADS = 16
PLAIN = 128
NF = 32
HEAD = PLAIN + 2 * NF
K = HEADS * HEAD
C = 2048
K_PASS = 4 * P
PASSES = K // K_PASS
N_BLOCK = 512
TOKEN_TILES = TOKENS // P
C_TILES = C // P
C_TILES_PER_BLOCK = N_BLOCK // P
C_BLOCKS = C // N_BLOCK

FLOPS = 2 * TOKENS * C * K
BYTES = 2 * C * K + 2 * TOKENS * K + 2 * POSITIONS * NF * 2 + 4 * TOKENS * C

LOADS = "g0 w0 w1 g1 w2 w3 w4 w5 g2 g3 w6 w7 w8 w9 w10 w11 w12 w13 w14 w15"
SCRIPT = "T:w0 T:w1 R:0c R:0s R:0a T:g0 Q:w0 T:w2 R:1c Q:w1 T:w3 R:1s Q:g0 R:1a T:g1 Q:w2 T:w4 Q:w3 T:w5 P:00 Q:g1 P:01 T:w6 R:2c Q:w4 T:w7 R:2s R:3c Q:w5 R:2a T:g2 R:3s Q:w6 R:3a T:g3 Q:w7 P:10 P:11 S:w8 T:w8 Q:g2 S:w9 T:w9 P:02 P:12 Q:g3 S:w10 T:w10 Q:w8 S:w11 T:w11 P:03 P:13 Q:w9 S:w12 T:w12 Q:w10 S:w13 T:w13 Q:w11 P:20 P:21 S:w14 T:w14 Q:w12 S:w15 T:w15 P:22 P:23 Q:w13 Q:w14 Q:w15 P:30 P:31 P:32 P:33"
W_CODE_BUFS = 3
GROUPED_BUFS = 3
T_BANKS = 6
RESULT_BUFS = 8
ROT_BUFS = 2
PAIRS = False
PAIR_BUFS = 2


def tile_fa3mlaattention_pb_kernel(tc, x, freqs_cis, w_q, grad_out, out):
    nc = tc.nc
    g_dram = grad_out.rearrange("b t h d -> (b t) (h d)")
    out_dram = out.rearrange("b t c -> (b t) c")

    with ExitStack() as ctx:
        ctx.enter_context(tc.manual_schedule())
        keep = ctx.enter_context(tc.tile_pool(name="keep", bufs=1))
        stage = ctx.enter_context(tc.tile_pool(name="stage", bufs=2))
        banks = ctx.enter_context(tc.psum_pool(name="banks", bufs=T_BANKS))
        sums = ctx.enter_context(tc.psum_pool(name="sums", bufs=8 - T_BANKS))

        freqs = keep.tile([P, POSITIONS // P, NF, 2], BF16)
        nc.sync.dma_start(out=freqs[:], in_=freqs_cis.rearrange("(a p) j s -> p a j s", p=P))
        g_rows = keep.tile([P, TOKEN_TILES, K], BF16)
        rows = {}
        for t in LOADS.split():
            i = int(t[1:3]) if t[0] == "w" else int(t[1])
            if t[0] == "g":
                cols = {"": slice(0, K), "A": slice(0, K // 2), "B": slice(K // 2, K)}[t[2:]]
                nc.sync.dma_start(out=g_rows[:, i, cols], in_=g_dram[i * P : (i + 1) * P, cols])
                rows[t[:2]] = g_rows[:, i, :]
            else:
                w_rows = stage.tile([P, K], BF16, name="w_rows", bufs=C_TILES)
                nc.sync.dma_start(out=w_rows[:], in_=w_q[i * P : (i + 1) * P, :])
                rows[t] = w_rows[:]

        identity = keep.tile([P, P], F32)
        make_identity(nc, identity[:])

        gq_codes = keep.tile([P, TOKEN_TILES, PASSES, P], U32, align_bytes=64)
        gq_scales = keep.tile([P, TOKEN_TILES, PASSES, P], U8, align_bytes=64)
        w_codes = {}
        w_scales = {}
        words = {}
        grouped = {}
        partial = {}
        shape = [P, HEADS, 2, NF]

        def rotated_of(tt):
            return g_rows[:, tt, :].rearrange("p (h d) -> p h d", d=HEAD)[:, :, PLAIN:HEAD].rearrange(
                "p h (f j) -> p h f j", f=2
            )

        def rotate_step(tt, step, half):
            a = tt % (POSITIONS // P)
            heads = {"": slice(0, HEADS), "A": slice(0, HEADS // 2), "B": slice(HEADS // 2, HEADS)}[half]
            rotated = rotated_of(tt)[:, heads, :, :]
            part = [P, HEADS if half == "" else HEADS // 2, 2, NF]
            if step == "c":
                if (tt, 0) not in partial:
                    partial[(tt, 0)] = stage.tile(shape, F32, name="by_cos", bufs=ROT_BUFS)
                cos = freqs[:, a, :, 0].unsqueeze(1).unsqueeze(1).to_broadcast(part)
                nc.vector.tensor_mul(out=partial[(tt, 0)][:, heads, :, :], in0=rotated, in1=cos)
            if step == "s":
                if (tt, 1) not in partial:
                    partial[(tt, 1)] = stage.tile(shape, F32, name="by_sin", bufs=ROT_BUFS)
                sin = freqs[:, a, :, 1].unsqueeze(1).unsqueeze(1).to_broadcast(part)
                nc.vector.tensor_mul(out=partial[(tt, 1)][:, heads, :, :], in0=rotated, in1=sin)
            if step == "a":
                by_cos, by_sin = partial[(tt, 0)], partial[(tt, 1)]
                nc.vector.tensor_add(out=rotated[:, :, 0, :], in0=by_cos[:, heads, 0, :], in1=by_sin[:, heads, 1, :])
                nc.vector.tensor_sub(out=rotated[:, :, 1, :], in0=by_cos[:, heads, 1, :], in1=by_sin[:, heads, 0, :])

        def sort_words(t, engine):
            w_sorted = stage.tile([P, 2, K // 4], F32, name="w_rows", bufs=C_TILES)
            src = rows[t].bitcast(F32).rearrange("p (w u) -> p u w", u=2)
            if engine == "D":
                nc.vector.tensor_copy(out=w_sorted[:], in_=src)
            else:
                nc.scalar.copy(out=w_sorted[:], in_=src)
            words[t] = w_sorted[:].rearrange("p u (g w) -> p g u w", g=PASSES)

        def transpose(t, engines):
            if t not in words:
                words[t] = rows[t].bitcast(F32).rearrange("p (g w u) -> p g u w", g=PASSES, u=2)
            if t[0] == "w" and PAIRS:
                pair, j = divmod(int(t[1:]), 2)
                if ("pair", pair) not in grouped:
                    grouped[("pair", pair)] = stage.tile([P, PASSES, 2, 4 * P], BF16, align_bytes=64, name="grouped_pair", bufs=PAIR_BUFS)
                grouped[t] = grouped[("pair", pair)][:, :, j, :]
            else:
                g_tile = stage.tile([P, PASSES, 4 * P], BF16, align_bytes=64, name="grouped", bufs=GROUPED_BUFS)
                grouped[t] = g_tile[:]
            grouped_words = grouped[t].bitcast(F32).rearrange("p g (r u) -> p g r u", u=2)
            for b in range(PASSES // 2):
                bank = banks.tile([P, 2, 2, P], F32)
                for g in range(2):
                    for u in range(2):
                        nc.tensor.transpose(bank[:, g, u, :], words[t][:, 2 * b + g, u, :], identity[:])
                dst = grouped_words[:, 2 * b : 2 * b + 2, :, :]
                src = bank[:].rearrange("p g u r -> p g r u")
                if engines[b] == "D":
                    nc.vector.tensor_copy(out=dst, in_=src)
                else:
                    nc.scalar.copy(out=dst, in_=src)

        def quantise(t):
            i = int(t[1:])
            if t[0] == "w":
                cb, j = divmod(i, C_TILES_PER_BLOCK)
                if cb not in w_codes:
                    w_codes[cb] = stage.tile([P, PASSES, N_BLOCK], U32, align_bytes=64, name="w_codes", bufs=W_CODE_BUFS)
                    w_scales[cb] = stage.tile([P, PASSES, N_BLOCK], U8, align_bytes=64, name="w_scales", bufs=W_CODE_BUFS)
                n = 2 if PAIRS else 1
                cols = slice(j * P, (j + n) * P)
                for g in range(PASSES):
                    nc.vector.quantize_mx(
                        out=w_codes[cb][:, g, cols].bitcast(E4M3_X4),
                        scales=w_scales[cb][:, g, cols],
                        in_=grouped[("pair", i // 2)][:, g, :, :].rearrange("p j e -> p (j e)") if PAIRS else grouped[t][:, g, :],
                    )
            else:
                for b in range(PASSES // 2):
                    two = slice(2 * b, 2 * b + 2)
                    nc.vector.quantize_mx(
                        out=gq_codes[:, i, two, :].rearrange("p g r -> p (g r)").bitcast(E5M2_X4),
                        scales=gq_scales[:, i, two, :].rearrange("p g r -> p (g r)"),
                        in_=grouped[t][:, two, :].rearrange("p g e -> p (g e)"),
                    )

        def product(cb, tt, engine):
            acc = sums.tile([P, N_BLOCK], F32)
            for g in range(PASSES):
                nc.tensor.matmul_mx(
                    out=acc[:],
                    lhsT=gq_codes[:, tt, g, :].bitcast(E5M2_X4),
                    lhsT_scale=gq_scales[:, tt, g, :],
                    rhs=w_codes[cb][:, g, :].bitcast(E4M3_X4),
                    rhs_scale=w_scales[cb][:, g, :],
                    start=(g == 0),
                    stop=(g == PASSES - 1),
                )
            result = stage.tile([P, N_BLOCK], F32, name="result", bufs=RESULT_BUFS)
            pieces = 2 if engine == "H" else 1
            width = N_BLOCK // pieces
            for h in range(pieces):
                cols = slice(h * width, (h + 1) * width)
                if engine == "D":
                    nc.vector.tensor_copy(out=result[:, cols], in_=acc[:, cols])
                else:
                    nc.scalar.copy(out=result[:, cols], in_=acc[:, cols])
                nc.sync.dma_start(
                    out=out_dram[tt * P : (tt + 1) * P, cb * N_BLOCK + h * width : cb * N_BLOCK + (h + 1) * width],
                    in_=result[:, cols],
                )

        for tok in SCRIPT.split():
            f = tok.split(":")
            if f[0] == "R":
                rotate_step(int(f[1][0]), f[1][1], f[1][2:])
            elif f[0] == "S":
                sort_words(f[1], f[2] if len(f) > 2 else "D")
            elif f[0] == "T":
                transpose(f[1], f[2] if len(f) > 2 else "AAA")
            elif f[0] == "Q":
                quantise(f[1])
            elif f[0] == "P":
                product(int(f[1][0]), int(f[1][1]), f[2] if len(f) > 2 else "A")
